import numpy as np
import ml_dtypes


def mxq(x, axis, fmt="e4m3"):
    dtype, down = {"e4m3": (ml_dtypes.float8_e4m3fn, 7), "e5m2": (ml_dtypes.float8_e5m2, 14)}[fmt]
    v = np.moveaxis(np.asarray(x, np.float32).astype(ml_dtypes.bfloat16).astype(np.float64), axis, -1)
    blocks = v.reshape(v.shape[:-1] + (-1, 32))
    amax = np.abs(blocks).max(-1, keepdims=True)
    byte = np.maximum(np.where(amax > 0, np.frexp(amax)[1] - 1 + 127, 0) - down, 1)
    scale = np.exp2(byte - 127.0)
    codes = (blocks / scale).astype(np.float32).astype(dtype).astype(np.float64)
    return np.moveaxis((codes * scale).reshape(v.shape), -1, axis)


WIDE = False


def mx_kscale(k):
    if not WIDE:
        return np.ones(k)
    levels = np.array([10, -10, 5, -5, 0])
    a = np.random.permutation(np.resize(levels, k // 512 * 4)).reshape(k // 512, 4)
    idx = np.arange(k)
    return np.exp2(a[idx // 512, idx % 128 // 32])


BF16 = ml_dtypes.bfloat16


def bf(x):
    return np.asarray(x, np.float32).astype(BF16)


def f64(x):
    return np.asarray(x).astype(np.float64)


E2M1 = np.array([0.0, 0.5, 1.0, 1.5, 2.0, 3.0, 4.0, 6.0, -0.0, -0.5, -1.0, -1.5, -2.0, -3.0, -4.0, -6.0])


def pack_weight(w, fmt):
    k, n = w.shape
    w = f64(bf(w)).reshape(k // 32, 32, n)
    amax = np.abs(w).max(1)
    if fmt == "e4m3":
        byte = np.frexp(amax)[1] - 1 + 127 - 7
    else:
        mant, ex = np.frexp(amax / 6.0)
        byte = np.where(mant > 0.5, ex, ex - 1) + 127
    byte = np.clip(np.where(amax > 0, byte, 1), 1, 254)
    scaled = (w * np.exp2(127.0 - byte)[:, None, :]).reshape(k, n).astype(np.float32)
    by_word = np.ascontiguousarray(scaled.reshape(k // 512, 128, 4, n).transpose(0, 1, 3, 2))
    if fmt == "e4m3":
        words = by_word.astype(ml_dtypes.float8_e4m3fn).view(np.uint8)
    else:
        c = by_word.astype(ml_dtypes.float4_e2m1fn).view(np.uint8) & 0xF
        words = c[..., 0::2] | (c[..., 1::2] << 4)
    return np.ascontiguousarray(words), np.ascontiguousarray(byte.astype(np.uint8).reshape(k // 512, 16, n))


def unpack_weight(words, scales, fmt):
    g, p, n, _ = words.shape
    if fmt == "e4m3":
        vals = np.ascontiguousarray(words).view(ml_dtypes.float8_e4m3fn).astype(np.float64)
    else:
        nib = np.empty((g, p, n, 4), np.uint8)
        nib[..., 0::2] = words & 0xF
        nib[..., 1::2] = words >> 4
        vals = E2M1[nib]
    vals = vals * np.repeat(np.exp2(scales.astype(np.float64) - 127.0), 8, axis=1)[..., None]
    return vals.transpose(0, 1, 3, 2).reshape(g * 512, n)


B, I, H = 128, 8192, 512


def sig(v):
    return 1.0 / (1.0 + np.exp(-v))


def setup_inputs():
    s, t = mx_kscale(I), mx_kscale(H)
    x = bf(np.random.standard_normal((B, I)) * s)
    m_prev = bf(np.random.standard_normal((B, H)) * t)
    c_prev = bf(np.random.standard_normal((B, H)))
    w_m_words, w_m_scales = pack_weight(np.random.standard_normal((H, 8 * H)) / np.sqrt(H) / t[:, None], "e4m3")
    w_inputs_words, w_inputs_scales = pack_weight(np.random.standard_normal((I, 8 * H)) / np.sqrt(I) / s[:, None], "e4m3")
    return {"x": x,
            "m_prev": m_prev,
            "c_prev": c_prev,
            "w_m_words": w_m_words,
            "w_m_scales": w_m_scales,
            "w_inputs_words": w_inputs_words,
            "w_inputs_scales": w_inputs_scales}


def reference(x, m_prev, c_prev, w_m_words, w_m_scales, w_inputs_words, w_inputs_scales):
    m_mat = mxq(f64(m_prev), 1, "e4m3") @ unpack_weight(w_m_words, w_m_scales, "e4m3")
    in_mat = mxq(f64(x), 1, "e4m3") @ unpack_weight(w_inputs_words, w_inputs_scales, "e4m3")
    ms = np.split(m_mat, 8, axis=1)
    xs = np.split(in_mat, 8, axis=1)
    l1_0 = sig(xs[0] + ms[0])
    l1_1 = np.maximum(xs[1] + ms[1], 0.0)
    l1_2 = sig(xs[2] + ms[2])
    l1_3 = np.maximum(xs[3] * ms[3], 0.0)
    l1_4 = np.tanh(xs[4] + ms[4])
    l1_5 = sig(xs[5] + ms[5])
    l1_6 = np.tanh(xs[6] + ms[6])
    l1_7 = sig(xs[7] + ms[7])
    l2_0 = np.tanh(l1_0 * l1_1)
    l2_1 = np.tanh(l1_2 + l1_3)
    l2_2 = np.tanh(l1_4 * l1_5)
    l2_3 = sig(l1_6 + l1_7)
    l2_0 = np.tanh(l2_0 + f64(c_prev))
    new_c = l2_0 * l2_1
    l3_1 = np.tanh(l2_2 + l2_3)
    new_m = np.tanh(new_c * l3_1)
    return (new_m, new_c)

@@ -1,0 +1,230 @@
+from contextlib import ExitStack
+
+import concourse.mybir as mybir
+from concourse.masks import make_identity
+
+F32 = mybir.dt.float32
+BF16 = mybir.dt.bfloat16
+I32 = mybir.dt.int32
+U32 = mybir.dt.uint32
+U8 = mybir.dt.uint8
+FP8X4 = mybir.dt.float8_e4m3fn_x4
+ACT = mybir.ActivationFunctionType
+ALU = mybir.AluOpType
+
+P = 128
+PACK = 4
+K_PASS = P * PACK
+WORDS = K_PASS // 2
+IN_DIM = 8192
+X_GROUPS = IN_DIM // K_PASS
+HIDDEN = 512
+PIECE = 512
+PIECES = 8
+N_ALL = PIECES * PIECE
+ROUND = 4
+PRODUCT_PIECE = 3
+PLANES = 4
+QUADRANTS = 4
+X_LOADS = 4
+W_BUFS = 12
+
+FLOPS = 2 * P * (IN_DIM + HIDDEN) * N_ALL
+
+
+def transpose_and_quantise(nc, bank, grouped_pool, copy_out, ident, src_words, codes, scales):
+    n_groups = src_words.shape[1] // WORDS
+    for g in range(n_groups):
+        for u in range(2):
+            slot = 2 * g + u
+            nc.tensor.transpose(
+                bank[:, slot * P : (slot + 1) * P],
+                src_words[:, g * WORDS + u : (g + 1) * WORDS : 2],
+                ident,
+            )
+    grouped = grouped_pool.tile([P, n_groups, P, PACK], BF16, align_bytes=64)
+    copy_out(
+        out=grouped[:].bitcast(F32),
+        in_=bank[:, : n_groups * 2 * P].rearrange("p (g u b) -> p g b u", g=n_groups, u=2),
+    )
+    nc.vector.quantize_mx(
+        out=codes.bitcast(FP8X4),
+        scales=scales,
+        in_=grouped[:].rearrange("p g b t -> p (g b t)"),
+    )
+
+
+def tile_nascell_k_kernel(
+    tc, x, m_prev, c_prev, w_m_words, w_m_scales, w_inputs_words, w_inputs_scales, out_0, out_1
+):
+    nc = tc.nc
+    with ExitStack() as ctx:
+        keep = ctx.enter_context(tc.tile_pool(name="keep", bufs=1))
+        grouped_pool = ctx.enter_context(tc.tile_pool(name="grouped", bufs=4))
+        word_pool = ctx.enter_context(tc.tile_pool(name="words", bufs=W_BUFS))
+        psum = ctx.enter_context(tc.psum_pool(name="psum", bufs=1))
+
+        x_planes = []
+        for i in range(X_GROUPS // PLANES):
+            planes = keep.tile([P, N_ALL], U8, name="x_planes%d" % i, align_bytes=64)
+            nc.vector.memset(planes[:].bitcast(I32), 0)
+            x_planes.append(planes)
+        m_planes = keep.tile([P, N_ALL // PLANES], U8, align_bytes=64)
+        nc.vector.memset(m_planes[:].bitcast(I32), 0)
+
+        ident = keep.tile([P, P], F32)
+        make_identity(nc, ident[:])
+
+        m_sb = keep.tile([P, HIDDEN], BF16)
+        nc.sync.dma_start(out=m_sb[:], in_=m_prev)
+        x_sb = keep.tile([P, IN_DIM], BF16)
+        for i in range(X_LOADS):
+            cols = slice(i * IN_DIM // X_LOADS, (i + 1) * IN_DIM // X_LOADS)
+            nc.sync.dma_start(out=x_sb[:, cols], in_=x[:, cols])
+        c_sb = keep.tile([P, HIDDEN], BF16)
+        nc.sync.dma_start(out=c_sb[:], in_=c_prev)
+
+        for quad in range(QUADRANTS):
+            rows = slice(PLANES * quad, PLANES * (quad + 1))
+            nc.sync.dma_start(
+                out=m_planes[32 * quad : 32 * quad + 16, :].bitcast(I32),
+                in_=w_m_scales[0, rows, :].rearrange("r (j n) -> j r n", j=PLANES).bitcast(I32),
+            )
+        for i in range(X_GROUPS // PLANES):
+            for quad in range(QUADRANTS):
+                rows = slice(PLANES * quad, PLANES * (quad + 1))
+                nc.sync.dma_start(
+                    out=x_planes[i][32 * quad : 32 * quad + 16, :].bitcast(I32),
+                    in_=w_inputs_scales[PLANES * i : PLANES * (i + 1), rows, :].bitcast(I32),
+                )
+
+        m_codes = keep.tile([P, P], U32, align_bytes=64)
+        m_scales = keep.tile([P, P], U8, align_bytes=64)
+        x_codes = keep.tile([P, X_GROUPS, P], U32, align_bytes=64)
+        x_scales = keep.tile([P, X_GROUPS, P], U8, align_bytes=64)
+
+        bank = psum.tile([P, PIECE], F32, tag="bank4", name="m_transposed")
+        transpose_and_quantise(
+            nc, bank, grouped_pool, nc.vector.tensor_copy, ident[:],
+            m_sb[:].bitcast(F32), m_codes[:], m_scales[:],
+        )
+        x_words = x_sb[:].bitcast(F32)
+        for step in range(X_GROUPS // 2):
+            pair = slice(2 * step, 2 * step + 2)
+            bank = psum.tile(
+                [P, PIECE], F32, tag="bank%d" % (5 + step % 3), name="x_transposed%d" % step
+            )
+            transpose_and_quantise(
+                nc, bank, grouped_pool,
+                nc.vector.tensor_copy if step % 2 == 0 else nc.scalar.copy,
+                ident[:],
+                x_words[:, 2 * step * WORDS : (2 * step + 2) * WORDS],
+                x_codes[:, pair, :].rearrange("p g b -> p (g b)"),
+                x_scales[:, pair, :].rearrange("p g b -> p (g b)"),
+            )
+
+        def load_words(group_words, first_piece):
+            words = word_pool.tile([P, ROUND * PIECE], U32, align_bytes=64)
+            first_byte = first_piece * PIECE * PACK
+            nc.sync.dma_start(
+                out=words[:].bitcast(I32),
+                in_=group_words.rearrange("p n t -> p (n t)")[
+                    :, first_byte : first_byte + ROUND * PIECE * PACK
+                ].bitcast(I32),
+            )
+            return words
+
+        def round_sums(first_piece, ms_product):
+            pieces = range(first_piece, first_piece + ROUND)
+            sums = {}
+            for piece in pieces:
+                sums[piece] = psum.tile(
+                    [P, PIECE], F32, tag="bank%d" % piece, name="sum%d" % piece
+                )
+            words = load_words(w_m_words[0], first_piece)
+            for piece in pieces:
+                alone = piece == PRODUCT_PIECE
+                plane = PLANES * (piece // 2)
+                nc.tensor.matmul_mx(
+                    out=ms_product[:] if alone else sums[piece][:],
+                    lhsT=m_codes[:].bitcast(FP8X4),
+                    lhsT_scale=m_scales[:],
+                    rhs=words[:, (piece - first_piece) * PIECE : (piece - first_piece + 1) * PIECE]
+                    .bitcast(FP8X4),
+                    rhs_scale=m_planes[plane:P, (piece % 2) * PIECE : (piece % 2 + 1) * PIECE],
+                    start=True,
+                    stop=alone,
+                )
+            for g in range(X_GROUPS):
+                words = load_words(w_inputs_words[g], first_piece)
+                plane = PLANES * (g % PLANES)
+                for piece in pieces:
+                    nc.tensor.matmul_mx(
+                        out=sums[piece][:],
+                        lhsT=x_codes[:, g, :].bitcast(FP8X4),
+                        lhsT_scale=x_scales[:, g, :],
+                        rhs=words[
+                            :, (piece - first_piece) * PIECE : (piece - first_piece + 1) * PIECE
+                        ].bitcast(FP8X4),
+                        rhs_scale=x_planes[g // PLANES][plane:P, piece * PIECE : (piece + 1) * PIECE],
+                        start=(g == 0 and piece == PRODUCT_PIECE),
+                        stop=(g == X_GROUPS - 1),
+                    )
+            return sums
+
+        def fresh(name):
+            return keep.tile([P, PIECE], F32, name=name)
+
+        def activate(name, func, in_):
+            result = fresh(name)
+            nc.scalar.activation(out=result[:], in_=in_[:], func=func)
+            return result
+
+        ms3_bank = psum.tile([P, PIECE], F32, tag="bank4", name="ms3_bank")
+        sums = round_sums(0, ms3_bank)
+        ms3 = fresh("ms3")
+        nc.scalar.copy(out=ms3[:], in_=ms3_bank[:])
+
+        l1_0 = activate("l1_0", ACT.Sigmoid, sums[0])
+        l1_01 = fresh("l1_01")
+        nc.vector.scalar_tensor_tensor(
+            out=l1_01[:], in0=sums[1][:], scalar=0.0, in1=l1_0[:], op0=ALU.max, op1=ALU.mult
+        )
+        l2_0_inner = activate("l2_0_inner", ACT.Tanh, l1_01)
+        with_c = fresh("with_c")
+        nc.vector.tensor_add(out=with_c[:], in0=l2_0_inner[:], in1=c_sb[:])
+        l2_0 = activate("l2_0", ACT.Tanh, with_c)
+
+        l1_2 = activate("l1_2", ACT.Sigmoid, sums[2])
+        product = fresh("product")
+        nc.vector.tensor_mul(out=product[:], in0=sums[3][:], in1=ms3[:])
+        l1_23 = fresh("l1_23")
+        nc.vector.scalar_tensor_tensor(
+            out=l1_23[:], in0=product[:], scalar=0.0, in1=l1_2[:], op0=ALU.max, op1=ALU.add
+        )
+        l2_1 = activate("l2_1", ACT.Tanh, l1_23)
+
+        new_c = fresh("new_c")
+        nc.vector.tensor_mul(out=new_c[:], in0=l2_0[:], in1=l2_1[:])
+        nc.scalar.dma_start(out=out_1, in_=new_c[:])
+
+        sums = round_sums(ROUND, None)
+        l1_4 = activate("l1_4", ACT.Tanh, sums[4])
+        l1_5 = activate("l1_5", ACT.Sigmoid, sums[5])
+        l1_45 = fresh("l1_45")
+        nc.vector.tensor_mul(out=l1_45[:], in0=l1_4[:], in1=l1_5[:])
+        l2_2 = activate("l2_2", ACT.Tanh, l1_45)
+
+        l1_6 = activate("l1_6", ACT.Tanh, sums[6])
+        l1_7 = activate("l1_7", ACT.Sigmoid, sums[7])
+        l1_67 = fresh("l1_67")
+        nc.vector.tensor_add(out=l1_67[:], in0=l1_6[:], in1=l1_7[:])
+        l2_3 = activate("l2_3", ACT.Sigmoid, l1_67)
+
+        l2_23 = fresh("l2_23")
+        nc.vector.tensor_add(out=l2_23[:], in0=l2_2[:], in1=l2_3[:])
+        l3_1 = activate("l3_1", ACT.Tanh, l2_23)
+        scaled_c = fresh("scaled_c")
+        nc.vector.tensor_mul(out=scaled_c[:], in0=new_c[:], in1=l3_1[:])
+        new_m = activate("new_m", ACT.Tanh, scaled_c)
+        nc.sync.dma_start(out=out_0, in_=new_m[:])

@@ -22,11 +22,11 @@ HIDDEN = 512
 PIECE = 512
 PIECES = 8
 N_ALL = PIECES * PIECE
-ROUND = 4
 PRODUCT_PIECE = 3
 PLANES = 4
 QUADRANTS = 4
 X_LOADS = 4
+TAIL_GROUPS = 4
 W_BUFS = 12
 
 FLOPS = 2 * P * (IN_DIM + HIDDEN) * N_ALL
@@ -103,7 +103,7 @@ def tile_nascell_k_kernel(
         x_codes = keep.tile([P, X_GROUPS, P], U32, align_bytes=64)
         x_scales = keep.tile([P, X_GROUPS, P], U8, align_bytes=64)
 
-        bank = psum.tile([P, PIECE], F32, tag="bank4", name="m_transposed")
+        bank = psum.tile([P, PIECE], F32, tag="bank0", name="m_transposed")
         transpose_and_quantise(
             nc, bank, grouped_pool, nc.vector.tensor_copy, ident[:],
             m_sb[:].bitcast(F32), m_codes[:], m_scales[:],
@@ -112,7 +112,7 @@ def tile_nascell_k_kernel(
         for step in range(X_GROUPS // 2):
             pair = slice(2 * step, 2 * step + 2)
             bank = psum.tile(
-                [P, PIECE], F32, tag="bank%d" % (5 + step % 3), name="x_transposed%d" % step
+                [P, PIECE], F32, tag="bank%d" % (1 + step % 7), name="x_transposed%d" % step
             )
             transpose_and_quantise(
                 nc, bank, grouped_pool,
@@ -123,108 +123,101 @@ def tile_nascell_k_kernel(
                 x_scales[:, pair, :].rearrange("p g b -> p (g b)"),
             )
 
-        def load_words(group_words, first_piece):
-            words = word_pool.tile([P, ROUND * PIECE], U32, align_bytes=64)
-            first_byte = first_piece * PIECE * PACK
-            nc.sync.dma_start(
-                out=words[:].bitcast(I32),
-                in_=group_words.rearrange("p n t -> p (n t)")[
-                    :, first_byte : first_byte + ROUND * PIECE * PACK
-                ].bitcast(I32),
+        def mx_pass(out, codes, scales, words, column, planes, start, stop):
+            nc.tensor.matmul_mx(
+                out=out[:],
+                lhsT=codes.bitcast(FP8X4),
+                lhsT_scale=scales,
+                rhs=words[:, column : column + PIECE].bitcast(FP8X4),
+                rhs_scale=planes,
+                start=start,
+                stop=stop,
             )
-            return words
 
-        def round_sums(first_piece, ms_product):
-            pieces = range(first_piece, first_piece + ROUND)
-            sums = {}
-            for piece in pieces:
-                sums[piece] = psum.tile(
-                    [P, PIECE], F32, tag="bank%d" % piece, name="sum%d" % piece
-                )
-            words = load_words(w_m_words[0], first_piece)
-            for piece in pieces:
-                alone = piece == PRODUCT_PIECE
-                plane = PLANES * (piece // 2)
-                nc.tensor.matmul_mx(
-                    out=ms_product[:] if alone else sums[piece][:],
-                    lhsT=m_codes[:].bitcast(FP8X4),
-                    lhsT_scale=m_scales[:],
-                    rhs=words[:, (piece - first_piece) * PIECE : (piece - first_piece + 1) * PIECE]
-                    .bitcast(FP8X4),
-                    rhs_scale=m_planes[plane:P, (piece % 2) * PIECE : (piece % 2 + 1) * PIECE],
-                    start=True,
-                    stop=alone,
-                )
-            for g in range(X_GROUPS):
-                words = load_words(w_inputs_words[g], first_piece)
-                plane = PLANES * (g % PLANES)
-                for piece in pieces:
-                    nc.tensor.matmul_mx(
-                        out=sums[piece][:],
-                        lhsT=x_codes[:, g, :].bitcast(FP8X4),
-                        lhsT_scale=x_scales[:, g, :],
-                        rhs=words[
-                            :, (piece - first_piece) * PIECE : (piece - first_piece + 1) * PIECE
-                        ].bitcast(FP8X4),
-                        rhs_scale=x_planes[g // PLANES][plane:P, piece * PIECE : (piece + 1) * PIECE],
-                        start=(g == 0 and piece == PRODUCT_PIECE),
-                        stop=(g == X_GROUPS - 1),
-                    )
-            return sums
+        m_words = keep.tile([P, N_ALL], U32, align_bytes=64)
+        nc.sync.dma_start(
+            out=m_words[:].bitcast(I32),
+            in_=w_m_words[0].rearrange("p n t -> p (n t)").bitcast(I32),
+        )
+        sums = {}
+        for piece in range(PIECES):
+            alone = piece == PRODUCT_PIECE
+            sums[piece] = psum.tile(
+                [P, PIECE], F32, tag="bank%d" % piece, name="ms3_bank" if alone else "sum%d" % piece
+            )
+            mx_pass(
+                sums[piece], m_codes[:], m_scales[:], m_words, piece * PIECE,
+                m_planes[PLANES * (piece // 2) : P, (piece % 2) * PIECE : (piece % 2 + 1) * PIECE],
+                start=True, stop=alone,
+            )
 
         def fresh(name):
             return keep.tile([P, PIECE], F32, name=name)
+
+        ms3 = fresh("ms3")
+        nc.scalar.copy(out=ms3[:], in_=sums[PRODUCT_PIECE][:])
+        sums[PRODUCT_PIECE] = psum.tile([P, PIECE], F32, tag="bank%d" % PRODUCT_PIECE, name="xs3")
+
+        def add_x_groups(groups, pieces):
+            first_byte = pieces[0] * PIECE * PACK
+            for g in groups:
+                words = word_pool.tile([P, len(pieces) * PIECE], U32, align_bytes=64)
+                nc.sync.dma_start(
+                    out=words[:].bitcast(I32),
+                    in_=w_inputs_words[g].rearrange("p n t -> p (n t)")[
+                        :, first_byte : first_byte + len(pieces) * PIECE * PACK
+                    ].bitcast(I32),
+                )
+                for piece in pieces:
+                    mx_pass(
+                        sums[piece], x_codes[:, g, :], x_scales[:, g, :],
+                        words, (piece - pieces[0]) * PIECE,
+                        x_planes[g // PLANES][
+                            PLANES * (g % PLANES) : P, piece * PIECE : (piece + 1) * PIECE
+                        ],
+                        start=(g == 0 and piece == PRODUCT_PIECE),
+                        stop=(g == X_GROUPS - 1),
+                    )
 
         def activate(name, func, in_):
             result = fresh(name)
             nc.scalar.activation(out=result[:], in_=in_[:], func=func)
             return result
 
-        ms3_bank = psum.tile([P, PIECE], F32, tag="bank4", name="ms3_bank")
-        sums = round_sums(0, ms3_bank)
-        ms3 = fresh("ms3")
-        nc.scalar.copy(out=ms3[:], in_=ms3_bank[:])
+        def combine(name, op, in0, in1):
+            result = fresh(name)
+            nc.vector.tensor_tensor(out=result[:], in0=in0[:], in1=in1[:], op=op)
+            return result
 
+        add_x_groups(range(X_GROUPS), [4, 5, 6, 7])
+        l1_4 = activate("l1_4", ACT.Tanh, sums[4])
+        l1_5 = activate("l1_5", ACT.Sigmoid, sums[5])
+        l2_2 = activate("l2_2", ACT.Tanh, combine("l1_45", ALU.mult, l1_4, l1_5))
+        l1_6 = activate("l1_6", ACT.Tanh, sums[6])
+        l1_7 = activate("l1_7", ACT.Sigmoid, sums[7])
+        l2_3 = activate("l2_3", ACT.Sigmoid, combine("l1_67", ALU.add, l1_6, l1_7))
+        l3_1 = activate("l3_1", ACT.Tanh, combine("l2_23", ALU.add, l2_2, l2_3))
+
+        add_x_groups(range(X_GROUPS - TAIL_GROUPS), [0, 1, 2, 3])
+        add_x_groups(range(X_GROUPS - TAIL_GROUPS, X_GROUPS), [0, 1])
         l1_0 = activate("l1_0", ACT.Sigmoid, sums[0])
         l1_01 = fresh("l1_01")
         nc.vector.scalar_tensor_tensor(
             out=l1_01[:], in0=sums[1][:], scalar=0.0, in1=l1_0[:], op0=ALU.max, op1=ALU.mult
         )
         l2_0_inner = activate("l2_0_inner", ACT.Tanh, l1_01)
-        with_c = fresh("with_c")
-        nc.vector.tensor_add(out=with_c[:], in0=l2_0_inner[:], in1=c_sb[:])
-        l2_0 = activate("l2_0", ACT.Tanh, with_c)
+        l2_0 = activate("l2_0", ACT.Tanh, combine("with_c", ALU.add, l2_0_inner, c_sb))
+        l2_0_l3_1 = combine("l2_0_l3_1", ALU.mult, l2_0, l3_1)
 
+        add_x_groups(range(X_GROUPS - TAIL_GROUPS, X_GROUPS), [2, 3])
         l1_2 = activate("l1_2", ACT.Sigmoid, sums[2])
-        product = fresh("product")
-        nc.vector.tensor_mul(out=product[:], in0=sums[3][:], in1=ms3[:])
+        product = combine("product", ALU.mult, sums[3], ms3)
         l1_23 = fresh("l1_23")
         nc.vector.scalar_tensor_tensor(
             out=l1_23[:], in0=product[:], scalar=0.0, in1=l1_2[:], op0=ALU.max, op1=ALU.add
         )
         l2_1 = activate("l2_1", ACT.Tanh, l1_23)
-
-        new_c = fresh("new_c")
-        nc.vector.tensor_mul(out=new_c[:], in0=l2_0[:], in1=l2_1[:])
-        nc.scalar.dma_start(out=out_1, in_=new_c[:])
-
-        sums = round_sums(ROUND, None)
-        l1_4 = activate("l1_4", ACT.Tanh, sums[4])
-        l1_5 = activate("l1_5", ACT.Sigmoid, sums[5])
-        l1_45 = fresh("l1_45")
-        nc.vector.tensor_mul(out=l1_45[:], in0=l1_4[:], in1=l1_5[:])
-        l2_2 = activate("l2_2", ACT.Tanh, l1_45)
-
-        l1_6 = activate("l1_6", ACT.Tanh, sums[6])
-        l1_7 = activate("l1_7", ACT.Sigmoid, sums[7])
-        l1_67 = fresh("l1_67")
-        nc.vector.tensor_add(out=l1_67[:], in0=l1_6[:], in1=l1_7[:])
-        l2_3 = activate("l2_3", ACT.Sigmoid, l1_67)
-
-        l2_23 = fresh("l2_23")
-        nc.vector.tensor_add(out=l2_23[:], in0=l2_2[:], in1=l2_3[:])
-        l3_1 = activate("l3_1", ACT.Tanh, l2_23)
-        scaled_c = fresh("scaled_c")
-        nc.vector.tensor_mul(out=scaled_c[:], in0=new_c[:], in1=l3_1[:])
-        new_m = activate("new_m", ACT.Tanh, scaled_c)
+        new_m = activate("new_m", ACT.Tanh, combine("scaled_c", ALU.mult, l2_0_l3_1, l2_1))
         nc.sync.dma_start(out=out_0, in_=new_m[:])
+        new_c = combine("new_c", ALU.mult, l2_0, l2_1)
+        nc.sync.dma_start(out=out_1, in_=new_c[:])

@@ -64,13 +64,13 @@ def tile_nascell_k_kernel(
         word_pool = ctx.enter_context(tc.tile_pool(name="words", bufs=W_BUFS))
         psum = ctx.enter_context(tc.psum_pool(name="psum", bufs=1))
 
-        x_planes = []
+        w_inputs_planes = []
         for i in range(X_GROUPS // PLANES):
-            planes = keep.tile([P, N_ALL], U8, name="x_planes%d" % i, align_bytes=64)
+            planes = keep.tile([P, N_ALL], U8, name="w_inputs_planes%d" % i, align_bytes=64)
             nc.vector.memset(planes[:].bitcast(I32), 0)
-            x_planes.append(planes)
-        m_planes = keep.tile([P, N_ALL // PLANES], U8, align_bytes=64)
-        nc.vector.memset(m_planes[:].bitcast(I32), 0)
+            w_inputs_planes.append(planes)
+        w_m_planes = keep.tile([P, N_ALL // PLANES], U8, align_bytes=64)
+        nc.vector.memset(w_m_planes[:].bitcast(I32), 0)
 
         ident = keep.tile([P, P], F32)
         make_identity(nc, ident[:])
@@ -86,16 +86,16 @@ def tile_nascell_k_kernel(
 
         for quad in range(QUADRANTS):
             rows = slice(PLANES * quad, PLANES * (quad + 1))
-            nc.sync.dma_start(
-                out=m_planes[32 * quad : 32 * quad + 16, :].bitcast(I32),
-                in_=w_m_scales[0, rows, :].rearrange("r (j n) -> j r n", j=PLANES).bitcast(I32),
+            nc.gpsimd.dma_start(
+                out=w_m_planes[32 * quad : 32 * quad + 16, :].bitcast(F32),
+                in_=w_m_scales[0, rows, :].rearrange("r (j n) -> j r n", j=PLANES).bitcast(F32),
             )
         for i in range(X_GROUPS // PLANES):
             for quad in range(QUADRANTS):
                 rows = slice(PLANES * quad, PLANES * (quad + 1))
-                nc.sync.dma_start(
-                    out=x_planes[i][32 * quad : 32 * quad + 16, :].bitcast(I32),
-                    in_=w_inputs_scales[PLANES * i : PLANES * (i + 1), rows, :].bitcast(I32),
+                nc.gpsimd.dma_start(
+                    out=w_inputs_planes[i][32 * quad : 32 * quad + 16, :].bitcast(F32),
+                    in_=w_inputs_scales[PLANES * i : PLANES * (i + 1), rows, :].bitcast(F32),
                 )
 
         m_codes = keep.tile([P, P], U32, align_bytes=64)
@@ -147,7 +147,7 @@ def tile_nascell_k_kernel(
             )
             mx_pass(
                 sums[piece], m_codes[:], m_scales[:], m_words, piece * PIECE,
-                m_planes[PLANES * (piece // 2) : P, (piece % 2) * PIECE : (piece % 2 + 1) * PIECE],
+                w_m_planes[PLANES * (piece // 2) : P, (piece % 2) * PIECE : (piece % 2 + 1) * PIECE],
                 start=True, stop=alone,
             )
 
@@ -172,7 +172,7 @@ def tile_nascell_k_kernel(
                     mx_pass(
                         sums[piece], x_codes[:, g, :], x_scales[:, g, :],
                         words, (piece - pieces[0]) * PIECE,
-                        x_planes[g // PLANES][
+                        w_inputs_planes[g // PLANES][
                             PLANES * (g % PLANES) : P, piece * PIECE : (piece + 1) * PIECE
                         ],
                         start=(g == 0 and piece == PRODUCT_PIECE),

@@ -158,7 +158,7 @@ def tile_nascell_k_kernel(
         nc.scalar.copy(out=ms3[:], in_=sums[PRODUCT_PIECE][:])
         sums[PRODUCT_PIECE] = psum.tile([P, PIECE], F32, tag="bank%d" % PRODUCT_PIECE, name="xs3")
 
-        def add_x_groups(groups, pieces):
+        def add_x_groups(groups, pieces, backwards=False):
             first_byte = pieces[0] * PIECE * PACK
             for g in groups:
                 words = word_pool.tile([P, len(pieces) * PIECE], U32, align_bytes=64)
@@ -168,7 +168,7 @@ def tile_nascell_k_kernel(
                         :, first_byte : first_byte + len(pieces) * PIECE * PACK
                     ].bitcast(I32),
                 )
-                for piece in pieces:
+                for piece in reversed(pieces) if backwards else pieces:
                     mx_pass(
                         sums[piece], x_codes[:, g, :], x_scales[:, g, :],
                         words, (piece - pieces[0]) * PIECE,
@@ -209,15 +209,28 @@ def tile_nascell_k_kernel(
         l2_0 = activate("l2_0", ACT.Tanh, combine("with_c", ALU.add, l2_0_inner, c_sb))
         l2_0_l3_1 = combine("l2_0_l3_1", ALU.mult, l2_0, l3_1)
 
-        add_x_groups(range(X_GROUPS - TAIL_GROUPS, X_GROUPS), [2, 3])
-        l1_2 = activate("l1_2", ACT.Sigmoid, sums[2])
-        product = combine("product", ALU.mult, sums[3], ms3)
+        add_x_groups(range(X_GROUPS - TAIL_GROUPS, X_GROUPS), [2, 3], backwards=True)
+        halves = [slice(0, PIECE // 2), slice(PIECE // 2, PIECE)]
+        product = fresh("product")
+        l1_2 = fresh("l1_2")
         l1_23 = fresh("l1_23")
-        nc.vector.scalar_tensor_tensor(
-            out=l1_23[:], in0=product[:], scalar=0.0, in1=l1_2[:], op0=ALU.max, op1=ALU.add
-        )
-        l2_1 = activate("l2_1", ACT.Tanh, l1_23)
-        new_m = activate("new_m", ACT.Tanh, combine("scaled_c", ALU.mult, l2_0_l3_1, l2_1))
-        nc.sync.dma_start(out=out_0, in_=new_m[:])
+        l2_1 = fresh("l2_1")
+        scaled_c = fresh("scaled_c")
+        new_m = fresh("new_m")
+        for h in halves:
+            nc.vector.tensor_tensor(out=product[:, h], in0=sums[3][:, h], in1=ms3[:, h], op=ALU.mult)
+        for h in halves:
+            nc.scalar.activation(out=l1_2[:, h], in_=sums[2][:, h], func=ACT.Sigmoid)
+        for h in halves:
+            nc.vector.scalar_tensor_tensor(
+                out=l1_23[:, h], in0=product[:, h], scalar=0.0, in1=l1_2[:, h], op0=ALU.max, op1=ALU.add
+            )
+        for h in halves:
+            nc.scalar.activation(out=l2_1[:, h], in_=l1_23[:, h], func=ACT.Tanh)
+        for h in halves:
+            nc.vector.tensor_tensor(out=scaled_c[:, h], in0=l2_0_l3_1[:, h], in1=l2_1[:, h], op=ALU.mult)
+        for h in halves:
+            nc.scalar.activation(out=new_m[:, h], in_=scaled_c[:, h], func=ACT.Tanh)
+            nc.sync.dma_start(out=out_0[:, h], in_=new_m[:, h])
         new_c = combine("new_c", ALU.mult, l2_0, l2_1)
         nc.sync.dma_start(out=out_1, in_=new_c[:])

@@ -27,7 +27,8 @@ PLANES = 4
 QUADRANTS = 4
 X_LOADS = 4
 TAIL_GROUPS = 4
-W_BUFS = 12
+WHOLE_GROUPS = 11
+W_BUFS = 7
 
 FLOPS = 2 * P * (IN_DIM + HIDDEN) * N_ALL
 
@@ -74,6 +75,10 @@ def tile_nascell_k_kernel(
 
         ident = keep.tile([P, P], F32)
         make_identity(nc, ident[:])
+
+        warm = keep.tile([P, 2], F32)
+        nc.vector.memset(warm[:], 0.0)
+        nc.scalar.activation(out=warm[:, 1:2], in_=warm[:, 0:1], func=ACT.Sigmoid)
 
         m_sb = keep.tile([P, HIDDEN], BF16)
         nc.sync.dma_start(out=m_sb[:], in_=m_prev)
@@ -134,7 +139,7 @@ def tile_nascell_k_kernel(
                 stop=stop,
             )
 
-        m_words = keep.tile([P, N_ALL], U32, align_bytes=64)
+        m_words = word_pool.tile([P, N_ALL], U32, tag="words", align_bytes=64)
         nc.sync.dma_start(
             out=m_words[:].bitcast(I32),
             in_=w_m_words[0].rearrange("p n t -> p (n t)").bitcast(I32),
@@ -161,7 +166,7 @@ def tile_nascell_k_kernel(
         def add_x_groups(groups, pieces, backwards=False):
             first_byte = pieces[0] * PIECE * PACK
             for g in groups:
-                words = word_pool.tile([P, len(pieces) * PIECE], U32, align_bytes=64)
+                words = word_pool.tile([P, len(pieces) * PIECE], U32, tag="words", align_bytes=64)
                 nc.sync.dma_start(
                     out=words[:].bitcast(I32),
                     in_=w_inputs_words[g].rearrange("p n t -> p (n t)")[
@@ -189,7 +194,8 @@ def tile_nascell_k_kernel(
             nc.vector.tensor_tensor(out=result[:], in0=in0[:], in1=in1[:], op=op)
             return result
 
-        add_x_groups(range(X_GROUPS), [4, 5, 6, 7])
+        add_x_groups(range(WHOLE_GROUPS), list(range(PIECES)))
+        add_x_groups(range(WHOLE_GROUPS, X_GROUPS), [4, 5, 6, 7])
         l1_4 = activate("l1_4", ACT.Tanh, sums[4])
         l1_5 = activate("l1_5", ACT.Sigmoid, sums[5])
         l2_2 = activate("l2_2", ACT.Tanh, combine("l1_45", ALU.mult, l1_4, l1_5))
@@ -198,7 +204,7 @@ def tile_nascell_k_kernel(
         l2_3 = activate("l2_3", ACT.Sigmoid, combine("l1_67", ALU.add, l1_6, l1_7))
         l3_1 = activate("l3_1", ACT.Tanh, combine("l2_23", ALU.add, l2_2, l2_3))
 
-        add_x_groups(range(X_GROUPS - TAIL_GROUPS), [0, 1, 2, 3])
+        add_x_groups(range(WHOLE_GROUPS, X_GROUPS - TAIL_GROUPS), [0, 1, 2, 3])
         add_x_groups(range(X_GROUPS - TAIL_GROUPS, X_GROUPS), [0, 1])
         l1_0 = activate("l1_0", ACT.Sigmoid, sums[0])
         l1_01 = fresh("l1_01")

@@ -206,17 +206,32 @@ def tile_nascell_k_kernel(
 
         add_x_groups(range(WHOLE_GROUPS, X_GROUPS - TAIL_GROUPS), [0, 1, 2, 3])
         add_x_groups(range(X_GROUPS - TAIL_GROUPS, X_GROUPS), [0, 1])
-        l1_0 = activate("l1_0", ACT.Sigmoid, sums[0])
+        blocks = [slice(i * PIECE // 4, (i + 1) * PIECE // 4) for i in range(4)]
+        l1_0 = fresh("l1_0")
         l1_01 = fresh("l1_01")
-        nc.vector.scalar_tensor_tensor(
-            out=l1_01[:], in0=sums[1][:], scalar=0.0, in1=l1_0[:], op0=ALU.max, op1=ALU.mult
-        )
-        l2_0_inner = activate("l2_0_inner", ACT.Tanh, l1_01)
-        l2_0 = activate("l2_0", ACT.Tanh, combine("with_c", ALU.add, l2_0_inner, c_sb))
-        l2_0_l3_1 = combine("l2_0_l3_1", ALU.mult, l2_0, l3_1)
+        l2_0_inner = fresh("l2_0_inner")
+        with_c = fresh("with_c")
+        l2_0 = fresh("l2_0")
+        l2_0_l3_1 = fresh("l2_0_l3_1")
+        for h in blocks:
+            nc.scalar.activation(out=l1_0[:, h], in_=sums[0][:, h], func=ACT.Sigmoid)
+        for h in blocks:
+            nc.vector.scalar_tensor_tensor(
+                out=l1_01[:, h], in0=sums[1][:, h], scalar=0.0, in1=l1_0[:, h], op0=ALU.max, op1=ALU.mult
+            )
+        for h in blocks:
+            nc.scalar.activation(out=l2_0_inner[:, h], in_=l1_01[:, h], func=ACT.Tanh)
+        for h in blocks:
+            nc.vector.tensor_tensor(out=with_c[:, h], in0=l2_0_inner[:, h], in1=c_sb[:, h], op=ALU.add)
+        for h in blocks:
+            nc.scalar.activation(out=l2_0[:, h], in_=with_c[:, h], func=ACT.Tanh)
+        for h in blocks:
+            nc.vector.tensor_tensor(out=l2_0_l3_1[:, h], in0=l2_0[:, h], in1=l3_1[:, h], op=ALU.mult)
 
-        add_x_groups(range(X_GROUPS - TAIL_GROUPS, X_GROUPS), [2, 3], backwards=True)
-        halves = [slice(0, PIECE // 2), slice(PIECE // 2, PIECE)]
+        add_x_groups(range(X_GROUPS - TAIL_GROUPS, X_GROUPS - 1), [2, 3], backwards=True)
+        add_x_groups([X_GROUPS - 1], [3])
+        add_x_groups([X_GROUPS - 1], [2])
+        halves = blocks
         product = fresh("product")
         l1_2 = fresh("l1_2")
         l1_23 = fresh("l1_23")

@@ -25,10 +25,11 @@ N_ALL = PIECES * PIECE
 PRODUCT_PIECE = 3
 PLANES = 4
 QUADRANTS = 4
-X_LOADS = 4
+X_LOADS = 1
 TAIL_GROUPS = 4
 WHOLE_GROUPS = 11
-W_BUFS = 7
+PAIRED_GROUPS = 10
+W_BUFS = 4
 
 FLOPS = 2 * P * (IN_DIM + HIDDEN) * N_ALL
 
@@ -184,6 +185,25 @@ def tile_nascell_k_kernel(
                         stop=(g == X_GROUPS - 1),
                     )
 
+        def add_x_group_pairs(groups):
+            for g0 in groups:
+                words = word_pool.tile([P, 2, N_ALL], U32, tag="words", align_bytes=64)
+                nc.sync.dma_start(
+                    out=words[:].bitcast(I32),
+                    in_=w_inputs_words[g0 : g0 + 2].rearrange("g p n t -> p g (n t)").bitcast(I32),
+                )
+                for g in (g0, g0 + 1):
+                    for piece in range(PIECES):
+                        mx_pass(
+                            sums[piece], x_codes[:, g, :], x_scales[:, g, :],
+                            words[:, g - g0, :], piece * PIECE,
+                            w_inputs_planes[g // PLANES][
+                                PLANES * (g % PLANES) : P, piece * PIECE : (piece + 1) * PIECE
+                            ],
+                            start=(g == 0 and piece == PRODUCT_PIECE),
+                            stop=False,
+                        )
+
         def activate(name, func, in_):
             result = fresh(name)
             nc.scalar.activation(out=result[:], in_=in_[:], func=func)
@@ -194,7 +214,8 @@ def tile_nascell_k_kernel(
             nc.vector.tensor_tensor(out=result[:], in0=in0[:], in1=in1[:], op=op)
             return result
 
-        add_x_groups(range(WHOLE_GROUPS), list(range(PIECES)))
+        add_x_group_pairs(range(0, PAIRED_GROUPS, 2))
+        add_x_groups(range(PAIRED_GROUPS, WHOLE_GROUPS), list(range(PIECES)))
         add_x_groups(range(WHOLE_GROUPS, X_GROUPS), [4, 5, 6, 7])
         l1_4 = activate("l1_4", ACT.Tanh, sums[4])
         l1_5 = activate("l1_5", ACT.Sigmoid, sums[5])

@@ -26,7 +26,7 @@ PRODUCT_PIECE = 3
 PLANES = 4
 QUADRANTS = 4
 X_LOADS = 1
-TAIL_GROUPS = 4
+TAIL_GROUPS = 3
 WHOLE_GROUPS = 11
 PAIRED_GROUPS = 10
 W_BUFS = 4

from contextlib import ExitStack

import concourse.mybir as mybir
from concourse.masks import make_identity

F32 = mybir.dt.float32
BF16 = mybir.dt.bfloat16
I32 = mybir.dt.int32
U32 = mybir.dt.uint32
U8 = mybir.dt.uint8
FP8X4 = mybir.dt.float8_e4m3fn_x4
ACT = mybir.ActivationFunctionType
ALU = mybir.AluOpType

P = 128
PACK = 4
K_PASS = P * PACK
WORDS = K_PASS // 2
IN_DIM = 8192
X_GROUPS = IN_DIM // K_PASS
HIDDEN = 512
PIECE = 512
PIECES = 8
N_ALL = PIECES * PIECE
PRODUCT_PIECE = 3
PLANES = 4
QUADRANTS = 4
X_LOADS = 1
TAIL_GROUPS = 3
WHOLE_GROUPS = 11
PAIRED_GROUPS = 10
W_BUFS = 4

FLOPS = 2 * P * (IN_DIM + HIDDEN) * N_ALL


def transpose_and_quantise(nc, bank, grouped_pool, copy_out, ident, src_words, codes, scales):
    n_groups = src_words.shape[1] // WORDS
    for g in range(n_groups):
        for u in range(2):
            slot = 2 * g + u
            nc.tensor.transpose(
                bank[:, slot * P : (slot + 1) * P],
                src_words[:, g * WORDS + u : (g + 1) * WORDS : 2],
                ident,
            )
    grouped = grouped_pool.tile([P, n_groups, P, PACK], BF16, align_bytes=64)
    copy_out(
        out=grouped[:].bitcast(F32),
        in_=bank[:, : n_groups * 2 * P].rearrange("p (g u b) -> p g b u", g=n_groups, u=2),
    )
    nc.vector.quantize_mx(
        out=codes.bitcast(FP8X4),
        scales=scales,
        in_=grouped[:].rearrange("p g b t -> p (g b t)"),
    )


def tile_nascell_k_kernel(
    tc, x, m_prev, c_prev, w_m_words, w_m_scales, w_inputs_words, w_inputs_scales, out_0, out_1
):
    nc = tc.nc
    with ExitStack() as ctx:
        keep = ctx.enter_context(tc.tile_pool(name="keep", bufs=1))
        grouped_pool = ctx.enter_context(tc.tile_pool(name="grouped", bufs=4))
        word_pool = ctx.enter_context(tc.tile_pool(name="words", bufs=W_BUFS))
        psum = ctx.enter_context(tc.psum_pool(name="psum", bufs=1))

        w_inputs_planes = []
        for i in range(X_GROUPS // PLANES):
            planes = keep.tile([P, N_ALL], U8, name="w_inputs_planes%d" % i, align_bytes=64)
            nc.vector.memset(planes[:].bitcast(I32), 0)
            w_inputs_planes.append(planes)
        w_m_planes = keep.tile([P, N_ALL // PLANES], U8, align_bytes=64)
        nc.vector.memset(w_m_planes[:].bitcast(I32), 0)

        ident = keep.tile([P, P], F32)
        make_identity(nc, ident[:])

        warm = keep.tile([P, 2], F32)
        nc.vector.memset(warm[:], 0.0)
        nc.scalar.activation(out=warm[:, 1:2], in_=warm[:, 0:1], func=ACT.Sigmoid)

        m_sb = keep.tile([P, HIDDEN], BF16)
        nc.sync.dma_start(out=m_sb[:], in_=m_prev)
        x_sb = keep.tile([P, IN_DIM], BF16)
        for i in range(X_LOADS):
            cols = slice(i * IN_DIM // X_LOADS, (i + 1) * IN_DIM // X_LOADS)
            nc.sync.dma_start(out=x_sb[:, cols], in_=x[:, cols])
        c_sb = keep.tile([P, HIDDEN], BF16)
        nc.sync.dma_start(out=c_sb[:], in_=c_prev)

        for quad in range(QUADRANTS):
            rows = slice(PLANES * quad, PLANES * (quad + 1))
            nc.gpsimd.dma_start(
                out=w_m_planes[32 * quad : 32 * quad + 16, :].bitcast(F32),
                in_=w_m_scales[0, rows, :].rearrange("r (j n) -> j r n", j=PLANES).bitcast(F32),
            )
        for i in range(X_GROUPS // PLANES):
            for quad in range(QUADRANTS):
                rows = slice(PLANES * quad, PLANES * (quad + 1))
                nc.gpsimd.dma_start(
                    out=w_inputs_planes[i][32 * quad : 32 * quad + 16, :].bitcast(F32),
                    in_=w_inputs_scales[PLANES * i : PLANES * (i + 1), rows, :].bitcast(F32),
                )

        m_codes = keep.tile([P, P], U32, align_bytes=64)
        m_scales = keep.tile([P, P], U8, align_bytes=64)
        x_codes = keep.tile([P, X_GROUPS, P], U32, align_bytes=64)
        x_scales = keep.tile([P, X_GROUPS, P], U8, align_bytes=64)

        bank = psum.tile([P, PIECE], F32, tag="bank0", name="m_transposed")
        transpose_and_quantise(
            nc, bank, grouped_pool, nc.vector.tensor_copy, ident[:],
            m_sb[:].bitcast(F32), m_codes[:], m_scales[:],
        )
        x_words = x_sb[:].bitcast(F32)
        for step in range(X_GROUPS // 2):
            pair = slice(2 * step, 2 * step + 2)
            bank = psum.tile(
                [P, PIECE], F32, tag="bank%d" % (1 + step % 7), name="x_transposed%d" % step
            )
            transpose_and_quantise(
                nc, bank, grouped_pool,
                nc.vector.tensor_copy if step % 2 == 0 else nc.scalar.copy,
                ident[:],
                x_words[:, 2 * step * WORDS : (2 * step + 2) * WORDS],
                x_codes[:, pair, :].rearrange("p g b -> p (g b)"),
                x_scales[:, pair, :].rearrange("p g b -> p (g b)"),
            )

        def mx_pass(out, codes, scales, words, column, planes, start, stop):
            nc.tensor.matmul_mx(
                out=out[:],
                lhsT=codes.bitcast(FP8X4),
                lhsT_scale=scales,
                rhs=words[:, column : column + PIECE].bitcast(FP8X4),
                rhs_scale=planes,
                start=start,
                stop=stop,
            )

        m_words = word_pool.tile([P, N_ALL], U32, tag="words", align_bytes=64)
        nc.sync.dma_start(
            out=m_words[:].bitcast(I32),
            in_=w_m_words[0].rearrange("p n t -> p (n t)").bitcast(I32),
        )
        sums = {}
        for piece in range(PIECES):
            alone = piece == PRODUCT_PIECE
            sums[piece] = psum.tile(
                [P, PIECE], F32, tag="bank%d" % piece, name="ms3_bank" if alone else "sum%d" % piece
            )
            mx_pass(
                sums[piece], m_codes[:], m_scales[:], m_words, piece * PIECE,
                w_m_planes[PLANES * (piece // 2) : P, (piece % 2) * PIECE : (piece % 2 + 1) * PIECE],
                start=True, stop=alone,
            )

        def fresh(name):
            return keep.tile([P, PIECE], F32, name=name)

        ms3 = fresh("ms3")
        nc.scalar.copy(out=ms3[:], in_=sums[PRODUCT_PIECE][:])
        sums[PRODUCT_PIECE] = psum.tile([P, PIECE], F32, tag="bank%d" % PRODUCT_PIECE, name="xs3")

        def add_x_groups(groups, pieces, backwards=False):
            first_byte = pieces[0] * PIECE * PACK
            for g in groups:
                words = word_pool.tile([P, len(pieces) * PIECE], U32, tag="words", align_bytes=64)
                nc.sync.dma_start(
                    out=words[:].bitcast(I32),
                    in_=w_inputs_words[g].rearrange("p n t -> p (n t)")[
                        :, first_byte : first_byte + len(pieces) * PIECE * PACK
                    ].bitcast(I32),
                )
                for piece in reversed(pieces) if backwards else pieces:
                    mx_pass(
                        sums[piece], x_codes[:, g, :], x_scales[:, g, :],
                        words, (piece - pieces[0]) * PIECE,
                        w_inputs_planes[g // PLANES][
                            PLANES * (g % PLANES) : P, piece * PIECE : (piece + 1) * PIECE
                        ],
                        start=(g == 0 and piece == PRODUCT_PIECE),
                        stop=(g == X_GROUPS - 1),
                    )

        def add_x_group_pairs(groups):
            for g0 in groups:
                words = word_pool.tile([P, 2, N_ALL], U32, tag="words", align_bytes=64)
                nc.sync.dma_start(
                    out=words[:].bitcast(I32),
                    in_=w_inputs_words[g0 : g0 + 2].rearrange("g p n t -> p g (n t)").bitcast(I32),
                )
                for g in (g0, g0 + 1):
                    for piece in range(PIECES):
                        mx_pass(
                            sums[piece], x_codes[:, g, :], x_scales[:, g, :],
                            words[:, g - g0, :], piece * PIECE,
                            w_inputs_planes[g // PLANES][
                                PLANES * (g % PLANES) : P, piece * PIECE : (piece + 1) * PIECE
                            ],
                            start=(g == 0 and piece == PRODUCT_PIECE),
                            stop=False,
                        )

        def activate(name, func, in_):
            result = fresh(name)
            nc.scalar.activation(out=result[:], in_=in_[:], func=func)
            return result

        def combine(name, op, in0, in1):
            result = fresh(name)
            nc.vector.tensor_tensor(out=result[:], in0=in0[:], in1=in1[:], op=op)
            return result

        add_x_group_pairs(range(0, PAIRED_GROUPS, 2))
        add_x_groups(range(PAIRED_GROUPS, WHOLE_GROUPS), list(range(PIECES)))
        add_x_groups(range(WHOLE_GROUPS, X_GROUPS), [4, 5, 6, 7])
        l1_4 = activate("l1_4", ACT.Tanh, sums[4])
        l1_5 = activate("l1_5", ACT.Sigmoid, sums[5])
        l2_2 = activate("l2_2", ACT.Tanh, combine("l1_45", ALU.mult, l1_4, l1_5))
        l1_6 = activate("l1_6", ACT.Tanh, sums[6])
        l1_7 = activate("l1_7", ACT.Sigmoid, sums[7])
        l2_3 = activate("l2_3", ACT.Sigmoid, combine("l1_67", ALU.add, l1_6, l1_7))
        l3_1 = activate("l3_1", ACT.Tanh, combine("l2_23", ALU.add, l2_2, l2_3))

        add_x_groups(range(WHOLE_GROUPS, X_GROUPS - TAIL_GROUPS), [0, 1, 2, 3])
        add_x_groups(range(X_GROUPS - TAIL_GROUPS, X_GROUPS), [0, 1])
        blocks = [slice(i * PIECE // 4, (i + 1) * PIECE // 4) for i in range(4)]
        l1_0 = fresh("l1_0")
        l1_01 = fresh("l1_01")
        l2_0_inner = fresh("l2_0_inner")
        with_c = fresh("with_c")
        l2_0 = fresh("l2_0")
        l2_0_l3_1 = fresh("l2_0_l3_1")
        for h in blocks:
            nc.scalar.activation(out=l1_0[:, h], in_=sums[0][:, h], func=ACT.Sigmoid)
        for h in blocks:
            nc.vector.scalar_tensor_tensor(
                out=l1_01[:, h], in0=sums[1][:, h], scalar=0.0, in1=l1_0[:, h], op0=ALU.max, op1=ALU.mult
            )
        for h in blocks:
            nc.scalar.activation(out=l2_0_inner[:, h], in_=l1_01[:, h], func=ACT.Tanh)
        for h in blocks:
            nc.vector.tensor_tensor(out=with_c[:, h], in0=l2_0_inner[:, h], in1=c_sb[:, h], op=ALU.add)
        for h in blocks:
            nc.scalar.activation(out=l2_0[:, h], in_=with_c[:, h], func=ACT.Tanh)
        for h in blocks:
            nc.vector.tensor_tensor(out=l2_0_l3_1[:, h], in0=l2_0[:, h], in1=l3_1[:, h], op=ALU.mult)

        add_x_groups(range(X_GROUPS - TAIL_GROUPS, X_GROUPS - 1), [2, 3], backwards=True)
        add_x_groups([X_GROUPS - 1], [3])
        add_x_groups([X_GROUPS - 1], [2])
        halves = blocks
        product = fresh("product")
        l1_2 = fresh("l1_2")
        l1_23 = fresh("l1_23")
        l2_1 = fresh("l2_1")
        scaled_c = fresh("scaled_c")
        new_m = fresh("new_m")
        for h in halves:
            nc.vector.tensor_tensor(out=product[:, h], in0=sums[3][:, h], in1=ms3[:, h], op=ALU.mult)
        for h in halves:
            nc.scalar.activation(out=l1_2[:, h], in_=sums[2][:, h], func=ACT.Sigmoid)
        for h in halves:
            nc.vector.scalar_tensor_tensor(
                out=l1_23[:, h], in0=product[:, h], scalar=0.0, in1=l1_2[:, h], op0=ALU.max, op1=ALU.add
            )
        for h in halves:
            nc.scalar.activation(out=l2_1[:, h], in_=l1_23[:, h], func=ACT.Tanh)
        for h in halves:
            nc.vector.tensor_tensor(out=scaled_c[:, h], in0=l2_0_l3_1[:, h], in1=l2_1[:, h], op=ALU.mult)
        for h in halves:
            nc.scalar.activation(out=new_m[:, h], in_=scaled_c[:, h], func=ACT.Tanh)
            nc.sync.dma_start(out=out_0[:, h], in_=new_m[:, h])
        new_c = combine("new_c", ALU.mult, l2_0, l2_1)
        nc.sync.dma_start(out=out_1, in_=new_c[:])
